import numpy as np
import ml_dtypes


def mxq(x, axis, fmt="e4m3"):
    dtype, down = {"e4m3": (ml_dtypes.float8_e4m3fn, 7), "e5m2": (ml_dtypes.float8_e5m2, 14)}[fmt]
    v = np.moveaxis(np.asarray(x, np.float32).astype(ml_dtypes.bfloat16).astype(np.float64), axis, -1)
    blocks = v.reshape(v.shape[:-1] + (-1, 32))
    amax = np.abs(blocks).max(-1, keepdims=True)
    byte = np.maximum(np.where(amax > 0, np.frexp(amax)[1] - 1 + 127, 0) - down, 1)
    scale = np.exp2(byte - 127.0)
    codes = (blocks / scale).astype(np.float32).astype(dtype).astype(np.float64)
    return np.moveaxis((codes * scale).reshape(v.shape), -1, axis)


WIDE = False


def mx_kscale(k):
    if not WIDE:
        return np.ones(k)
    levels = np.array([10, -10, 5, -5, 0])
    a = np.random.permutation(np.resize(levels, k // 512 * 4)).reshape(k // 512, 4)
    idx = np.arange(k)
    return np.exp2(a[idx // 512, idx % 128 // 32])


BF16 = ml_dtypes.bfloat16


def bf(x):
    return np.asarray(x, np.float32).astype(BF16)


def f64(x):
    return np.asarray(x).astype(np.float64)


I, M, O, B = 1024, 1024, 1024, 1024


def sigmoid(v):
    return 1.0 / (1.0 + np.exp(-v))


def setup_inputs():
    s, u, t = mx_kscale(I), mx_kscale(O), mx_kscale(M)
    return {
        "x": bf(np.random.standard_normal((I, B)) * s[:, None]),
        "out0": bf(np.tanh(np.random.standard_normal((O, B))) * u[:, None]),
        "mem0": bf(np.random.standard_normal((M, B)) * 0.8 * t[:, None]),
        "inp_out": bf(sigmoid(np.random.standard_normal((M, B)) * 1.2) * sigmoid(np.random.standard_normal((M, B)) * 1.4)),
        "w_readgate": bf(np.random.standard_normal((M, I)) / np.sqrt(I) / s),
        "w_rec_readgate": bf(np.random.standard_normal((M, O)) / np.sqrt(O) / u),
        "w_mem_readgate": bf(np.random.standard_normal((M, M)) / np.sqrt(M) / t),
        "w_hid_out": bf(np.random.standard_normal((O, M)) / np.sqrt(M)),
    }


def reference(x, out0, mem0, inp_out, w_readgate, w_rec_readgate, w_mem_readgate, w_hid_out):
    mem_out = sigmoid((mxq(f64(w_readgate), 1, "e4m3") @ mxq(f64(x), 0, "e4m3")) + (mxq(f64(w_rec_readgate), 1, "e4m3") @ mxq(f64(out0), 0, "e4m3")) + (mxq(f64(w_mem_readgate), 1, "e4m3") @ mxq(f64(mem0), 0, "e4m3")))
    hidden_act = mem_out + f64(inp_out)
    return np.tanh(mxq(f64(w_hid_out), 1, "e4m3") @ mxq(hidden_act, 0, "e4m3"))

@@ -1,0 +1,271 @@
+from contextlib import ExitStack
+
+import concourse.mybir as mybir
+from concourse.masks import make_identity
+
+F32 = mybir.dt.float32
+BF16 = mybir.dt.bfloat16
+U32 = mybir.dt.uint32
+U8 = mybir.dt.uint8
+FP8X4 = mybir.dt.float8_e4m3fn_x4
+ACTF = mybir.ActivationFunctionType
+ALU = mybir.AluOpType
+
+P = 128
+HALF = 512
+FLOPS = 4 * 2 * 1024 * 1024 * 1024
+PIN = True
+RAW_BUFS = 7
+
+
+def tile_pt_grumb_pb_kernel(
+    tc, x, out0, mem0, inp_out, w_readgate, w_rec_readgate, w_mem_readgate, w_hid_out, out
+):
+    nc = tc.nc
+    acts = [x, out0, mem0]
+    weights = [w_readgate, w_rec_readgate, w_mem_readgate, w_hid_out]
+    act_v = [a.rearrange("(g u p e) c -> g u p e c", g=2, u=2, e=2) for a in acts]
+    w_v = [w.rearrange("(G U p E) k -> G U p (E k)", G=2, U=2, E=2) for w in weights]
+    inp_v = inp_out.rearrange("(G U p E) c -> G U p (E c)", G=2, U=2, E=2)
+    out_v = out.rearrange("(G U p E) c -> G U E p c", G=2, U=2, E=2)
+
+    with ExitStack() as ctx:
+        if PIN:
+            ctx.enter_context(tc.manual_schedule())
+        const = ctx.enter_context(tc.tile_pool(name="const", bufs=1))
+        keep = ctx.enter_context(tc.tile_pool(name="keep", bufs=1))
+        rawp = ctx.enter_context(tc.tile_pool(name="rawp", bufs=RAW_BUFS))
+        agp = ctx.enter_context(tc.tile_pool(name="agp", bufs=3))
+        wgp = ctx.enter_context(tc.tile_pool(name="wgp", bufs=4))
+        sp = ctx.enter_context(tc.tile_pool(name="sp", bufs=2))
+        hgp = ctx.enter_context(tc.tile_pool(name="hgp", bufs=2))
+        op = ctx.enter_context(tc.tile_pool(name="op", bufs=6))
+        psum = ctx.enter_context(tc.psum_pool(name="psum", bufs=4))
+
+        ident = const.tile([P, P], F32, name="ident")
+        make_identity(nc, ident[:])
+        warm = const.tile([P, 8], F32, name="warm")
+        nc.vector.memset(warm[:], 0.0)
+        nc.scalar.activation(out=warm[:], in_=warm[:], func=ACTF.Sigmoid)
+
+        inp = keep.tile([P, 2, 4, 1024], BF16, name="inp")
+        a_codes = {}
+        a_scales = {}
+        h_codes = {}
+        h_scales = {}
+        for h in range(2):
+            for a in range(3):
+                a_codes[(a, h)] = keep.tile([P, 2, HALF], U32, name="ac%d%d" % (a, h), align_bytes=64)
+                a_scales[(a, h)] = keep.tile([P, 2, HALF], U8, name="as%d%d" % (a, h), align_bytes=64)
+            for G in range(2):
+                h_codes[(h, G)] = keep.tile([P, HALF], U32, name="hc%d%d" % (h, G), align_bytes=64)
+                h_scales[(h, G)] = keep.tile([P, HALF], U8, name="hs%d%d" % (h, G), align_bytes=64)
+        w_codes = {}
+        w_scales = {}
+        for w in range(4):
+            for G in range(2):
+                w_codes[(w, G)] = keep.tile([P, 4, 2, P], U32, name="wc%d%d" % (w, G), align_bytes=64)
+                w_scales[(w, G)] = keep.tile([P, 4, 2, P], U8, name="ws%d%d" % (w, G), align_bytes=64)
+
+        loads = [
+            ("a", 0, 0), ("w", 0, 0), ("a", 1, 0), ("w", 1, 0), ("a", 2, 0), ("w", 2, 0),
+            ("w", 0, 1), ("w", 1, 1), ("w", 2, 1), ("a", 0, 1), ("a", 1, 1), ("a", 2, 1),
+            ("w", 3, 0), ("w", 3, 1),
+        ]
+        raws = {}
+        nxt = [0]
+
+        def load_next():
+            if nxt[0] >= len(loads):
+                return
+            kind, i, j = loads[nxt[0]]
+            nxt[0] += 1
+            raw = rawp.tile([P, 4096], BF16, tag="raw", name="raw_%s%d%d" % (kind, i, j))
+            raws[(kind, i, j)] = raw
+            if kind == "a":
+                for g in range(2):
+                    for u in range(2):
+                        o = (4 * g + 2 * u) * HALF
+                        nc.sync.dma_start(
+                            out=raw[:, o:o + 2 * HALF].rearrange("p (e c) -> p e c", e=2),
+                            in_=act_v[i][g, u][:, :, j * HALF:(j + 1) * HALF],
+                        )
+                if (i, j) == (2, 1):
+                    for G in range(2):
+                        for U in range(2):
+                            nc.sync.dma_start(
+                                out=inp[:, G, 2 * U:2 * U + 2, :].rearrange("p t c -> p (t c)"),
+                                in_=inp_v[G, U],
+                            )
+            else:
+                for U in range(2):
+                    nc.sync.dma_start(out=raw[:, U * 2048:(U + 1) * 2048], in_=w_v[i][j, U])
+
+        def regroup(a, h, g):
+            raw = raws[("a", a, h)]
+            ag = agp.tile([P, 2048], BF16, tag="ag", name="ag%d%d%d" % (a, h, g), align_bytes=64)
+            nc.vector.tensor_copy(
+                out=ag[:].rearrange("p (c i t) -> p c t i", i=4, t=4),
+                in_=raw[:, g * 2048:(g + 1) * 2048].rearrange("p (t c i) -> p c t i", t=4, i=4),
+            )
+            return ag
+
+        def quant_act(a, h, g, ag):
+            nc.vector.quantize_mx(
+                out=a_codes[(a, h)][:, g, :].bitcast(FP8X4),
+                scales=a_scales[(a, h)][:, g, :],
+                in_=ag[:],
+            )
+
+        def prep_act(a, h):
+            ag0 = regroup(a, h, 0)
+            ag1 = regroup(a, h, 1)
+            quant_act(a, h, 0, ag0)
+            quant_act(a, h, 1, ag1)
+            load_next()
+
+        def transpose_w(w, G):
+            words = raws[("w", w, G)][:].bitcast(F32)
+            banks = []
+            for jj in range(4):
+                tb = psum.tile([P, 4, P], F32, tag="T", name="tb%d%d%d" % (w, G, jj))
+                for b in range(4):
+                    c0 = jj * 512 + b * P
+                    nc.tensor.transpose(tb[:, b, :], words[:, c0:c0 + P], ident[:])
+                banks.append(tb)
+            load_next()
+            wgs = []
+            for half in range(2):
+                wg = wgp.tile([P, 2048], BF16, tag="wg", name="wg%d%d%d" % (w, G, half), align_bytes=64)
+                wgf = wg[:].bitcast(F32).rearrange("p (a g m u) -> p a g m u", a=2, g=2, u=2)
+                for a2 in range(2):
+                    nc.scalar.copy(
+                        out=wgf[:, a2],
+                        in_=banks[2 * half + a2][:].rearrange("p (g u) m -> p g m u", u=2),
+                    )
+                wgs.append(wg)
+            return wgs
+
+        def quant_w(w, G, half, wg):
+            nc.vector.quantize_mx(
+                out=w_codes[(w, G)][:, 2 * half:2 * half + 2].rearrange("p a g m -> p (a g m)").bitcast(FP8X4),
+                scales=w_scales[(w, G)][:, 2 * half:2 * half + 2].rearrange("p a g m -> p (a g m)"),
+                in_=wg[:],
+            )
+
+        def prep_w(w, G):
+            wgs = transpose_w(w, G)
+            quant_w(w, G, 0, wgs[0])
+            quant_w(w, G, 1, wgs[1])
+
+        def open_accs(h, G):
+            return [psum.tile([P, HALF], F32, tag="acc", name="acc%d%d%d" % (h, G, jj)) for jj in range(4)]
+
+        def mx1(w, G, h, accs):
+            for jj in range(4):
+                for g in range(2):
+                    nc.tensor.matmul_mx(
+                        out=accs[jj][:],
+                        lhsT=w_codes[(w, G)][:, jj, g, :].bitcast(FP8X4),
+                        lhsT_scale=w_scales[(w, G)][:, jj, g, :],
+                        rhs=a_codes[(w, h)][:, g, :].bitcast(FP8X4),
+                        rhs_scale=a_scales[(w, h)][:, g, :],
+                        start=(w == 0 and g == 0),
+                        stop=(w == 2 and g == 1),
+                    )
+
+        def sigmoids(h, G, accs):
+            s = sp.tile([P, 4, HALF], F32, tag="s", name="s%d%d" % (h, G))
+            for jj in range(4):
+                nc.scalar.activation(out=s[:, jj, :], in_=accs[jj][:], func=ACTF.Sigmoid)
+            return s
+
+        def add_inp(h, G, s):
+            hg = hgp.tile([P, HALF, 4], BF16, tag="hg", name="hg%d%d" % (h, G), align_bytes=64)
+            nc.vector.tensor_tensor(
+                out=hg[:],
+                in0=s[:].rearrange("p t c -> p c t"),
+                in1=inp[:, G, :, h * HALF:(h + 1) * HALF].rearrange("p t c -> p c t"),
+                op=ALU.add,
+            )
+            return hg
+
+        def quant_h(h, G, hg):
+            nc.vector.quantize_mx(
+                out=h_codes[(h, G)][:].bitcast(FP8X4),
+                scales=h_scales[(h, G)][:],
+                in_=hg[:].rearrange("p c t -> p (c t)"),
+            )
+
+        def stage2(h):
+            for Go in range(2):
+                for jj in range(4):
+                    acc = psum.tile([P, HALF], F32, tag="acc", name="o_acc%d%d%d" % (h, Go, jj))
+                    for G in range(2):
+                        nc.tensor.matmul_mx(
+                            out=acc[:],
+                            lhsT=w_codes[(3, Go)][:, jj, G, :].bitcast(FP8X4),
+                            lhsT_scale=w_scales[(3, Go)][:, jj, G, :],
+                            rhs=h_codes[(h, G)][:].bitcast(FP8X4),
+                            rhs_scale=h_scales[(h, G)][:],
+                            start=(G == 0),
+                            stop=(G == 1),
+                        )
+                    o = op.tile([P, HALF], F32, tag="o", name="o%d%d%d" % (h, Go, jj))
+                    nc.scalar.activation(out=o[:], in_=acc[:], func=ACTF.Tanh)
+                    nc.sync.dma_start(out=out_v[Go, jj // 2, jj % 2][:, h * HALF:(h + 1) * HALF], in_=o[:])
+
+        for n in range(RAW_BUFS):
+            load_next()
+        prep_act(0, 0)
+        prep_w(0, 0)
+        prep_act(1, 0)
+        prep_w(1, 0)
+        acc00 = open_accs(0, 0)
+        mx1(0, 0, 0, acc00)
+        prep_act(2, 0)
+        prep_w(2, 0)
+        mx1(1, 0, 0, acc00)
+        prep_w(0, 1)
+        mx1(2, 0, 0, acc00)
+        s00 = sigmoids(0, 0, acc00)
+        prep_w(1, 1)
+        acc01 = open_accs(0, 1)
+        mx1(0, 1, 0, acc01)
+        wgs = transpose_w(2, 1)
+        ag0 = regroup(0, 1, 0)
+        quant_w(2, 1, 0, wgs[0])
+        ag1 = regroup(0, 1, 1)
+        quant_w(2, 1, 1, wgs[1])
+        quant_act(0, 1, 0, ag0)
+        quant_act(0, 1, 1, ag1)
+        load_next()
+        mx1(1, 1, 0, acc01)
+        mx1(2, 1, 0, acc01)
+        s01 = sigmoids(0, 1, acc01)
+        prep_act(1, 1)
+        acc10 = open_accs(1, 0)
+        mx1(0, 0, 1, acc10)
+        prep_act(2, 1)
+        hg00 = add_inp(0, 0, s00)
+        hg01 = add_inp(0, 1, s01)
+        quant_h(0, 0, hg00)
+        quant_h(0, 1, hg01)
+        mx1(1, 0, 1, acc10)
+        mx1(2, 0, 1, acc10)
+        s10 = sigmoids(1, 0, acc10)
+        acc11 = open_accs(1, 1)
+        mx1(0, 1, 1, acc11)
+        wgs0 = transpose_w(3, 0)
+        hg10 = add_inp(1, 0, s10)
+        quant_w(3, 0, 0, wgs0[0])
+        quant_w(3, 0, 1, wgs0[1])
+        quant_h(1, 0, hg10)
+        mx1(1, 1, 1, acc11)
+        prep_w(3, 1)
+        mx1(2, 1, 1, acc11)
+        s11 = sigmoids(1, 1, acc11)
+        hg11 = add_inp(1, 1, s11)
+        quant_h(1, 1, hg11)
+        stage2(0)
+        stage2(1)

@@ -14,7 +14,7 @@ ALU = mybir.AluOpType
 P = 128
 HALF = 512
 FLOPS = 4 * 2 * 1024 * 1024 * 1024
-PIN = True
+PIN = False
 RAW_BUFS = 7
 
 

@@ -14,7 +14,7 @@ ALU = mybir.AluOpType
 P = 128
 HALF = 512
 FLOPS = 4 * 2 * 1024 * 1024 * 1024
-PIN = False
+PIN = True
 RAW_BUFS = 7
 
 
@@ -37,7 +37,7 @@ def tile_pt_grumb_pb_kernel(
         rawp = ctx.enter_context(tc.tile_pool(name="rawp", bufs=RAW_BUFS))
         agp = ctx.enter_context(tc.tile_pool(name="agp", bufs=3))
         wgp = ctx.enter_context(tc.tile_pool(name="wgp", bufs=4))
-        sp = ctx.enter_context(tc.tile_pool(name="sp", bufs=2))
+        sp = ctx.enter_context(tc.tile_pool(name="sp", bufs=3))
         hgp = ctx.enter_context(tc.tile_pool(name="hgp", bufs=2))
         op = ctx.enter_context(tc.tile_pool(name="op", bufs=6))
         psum = ctx.enter_context(tc.psum_pool(name="psum", bufs=4))
@@ -101,13 +101,15 @@ def tile_pt_grumb_pb_kernel(
                 for U in range(2):
                     nc.sync.dma_start(out=raw[:, U * 2048:(U + 1) * 2048], in_=w_v[i][j, U])
 
-        def regroup(a, h, g):
+        def regroup(a, h, g, on_scalar=False):
             raw = raws[("a", a, h)]
             ag = agp.tile([P, 2048], BF16, tag="ag", name="ag%d%d%d" % (a, h, g), align_bytes=64)
-            nc.vector.tensor_copy(
-                out=ag[:].rearrange("p (c i t) -> p c t i", i=4, t=4),
-                in_=raw[:, g * 2048:(g + 1) * 2048].rearrange("p (t c i) -> p c t i", t=4, i=4),
-            )
+            dst = ag[:].rearrange("p (c i t) -> p c t i", i=4, t=4)
+            src = raw[:, g * 2048:(g + 1) * 2048].rearrange("p (t c i) -> p c t i", t=4, i=4)
+            if on_scalar:
+                nc.scalar.copy(out=dst, in_=src)
+            else:
+                nc.vector.tensor_copy(out=dst, in_=src)
             return ag
 
         def quant_act(a, h, g, ag):
@@ -124,7 +126,7 @@ def tile_pt_grumb_pb_kernel(
             quant_act(a, h, 1, ag1)
             load_next()
 
-        def transpose_w(w, G):
+        def transpose_w(w, G, share=False):
             words = raws[("w", w, G)][:].bitcast(F32)
             banks = []
             for jj in range(4):
@@ -139,10 +141,11 @@ def tile_pt_grumb_pb_kernel(
                 wg = wgp.tile([P, 2048], BF16, tag="wg", name="wg%d%d%d" % (w, G, half), align_bytes=64)
                 wgf = wg[:].bitcast(F32).rearrange("p (a g m u) -> p a g m u", a=2, g=2, u=2)
                 for a2 in range(2):
-                    nc.scalar.copy(
-                        out=wgf[:, a2],
-                        in_=banks[2 * half + a2][:].rearrange("p (g u) m -> p g m u", u=2),
-                    )
+                    bank = banks[2 * half + a2][:].rearrange("p (g u) m -> p g m u", u=2)
+                    if share and a2 == 1:
+                        nc.vector.tensor_copy(out=wgf[:, a2], in_=bank)
+                    else:
+                        nc.scalar.copy(out=wgf[:, a2], in_=bank)
                 wgs.append(wg)
             return wgs
 
@@ -153,8 +156,8 @@ def tile_pt_grumb_pb_kernel(
                 in_=wg[:],
             )
 
-        def prep_w(w, G):
-            wgs = transpose_w(w, G)
+        def prep_w(w, G, share=False):
+            wgs = transpose_w(w, G, share)
             quant_w(w, G, 0, wgs[0])
             quant_w(w, G, 1, wgs[1])
 
@@ -183,9 +186,9 @@ def tile_pt_grumb_pb_kernel(
         def add_inp(h, G, s):
             hg = hgp.tile([P, HALF, 4], BF16, tag="hg", name="hg%d%d" % (h, G), align_bytes=64)
             nc.vector.tensor_tensor(
-                out=hg[:],
-                in0=s[:].rearrange("p t c -> p c t"),
-                in1=inp[:, G, :, h * HALF:(h + 1) * HALF].rearrange("p t c -> p c t"),
+                out=hg[:].rearrange("p (c i) t -> p c t i", i=4),
+                in0=s[:].rearrange("p t (c i) -> p c t i", i=4),
+                in1=inp[:, G, :, h * HALF:(h + 1) * HALF].rearrange("p t (c i) -> p c t i", i=4),
                 op=ALU.add,
             )
             return hg
@@ -217,15 +220,15 @@ def tile_pt_grumb_pb_kernel(
 
         for n in range(RAW_BUFS):
             load_next()
+        acc00 = open_accs(0, 0)
         prep_act(0, 0)
         prep_w(0, 0)
+        mx1(0, 0, 0, acc00)
         prep_act(1, 0)
         prep_w(1, 0)
-        acc00 = open_accs(0, 0)
-        mx1(0, 0, 0, acc00)
+        mx1(1, 0, 0, acc00)
         prep_act(2, 0)
         prep_w(2, 0)
-        mx1(1, 0, 0, acc00)
         prep_w(0, 1)
         mx1(2, 0, 0, acc00)
         s00 = sigmoids(0, 0, acc00)
@@ -246,7 +249,11 @@ def tile_pt_grumb_pb_kernel(
         prep_act(1, 1)
         acc10 = open_accs(1, 0)
         mx1(0, 0, 1, acc10)
-        prep_act(2, 1)
+        ag0 = regroup(2, 1, 0)
+        ag1 = regroup(2, 1, 1, True)
+        quant_act(2, 1, 0, ag0)
+        quant_act(2, 1, 1, ag1)
+        load_next()
         hg00 = add_inp(0, 0, s00)
         hg01 = add_inp(0, 1, s01)
         quant_h(0, 0, hg00)
@@ -256,13 +263,13 @@ def tile_pt_grumb_pb_kernel(
         s10 = sigmoids(1, 0, acc10)
         acc11 = open_accs(1, 1)
         mx1(0, 1, 1, acc11)
-        wgs0 = transpose_w(3, 0)
+        wgs0 = transpose_w(3, 0, True)
         hg10 = add_inp(1, 0, s10)
         quant_w(3, 0, 0, wgs0[0])
         quant_w(3, 0, 1, wgs0[1])
         quant_h(1, 0, hg10)
         mx1(1, 1, 1, acc11)
-        prep_w(3, 1)
+        prep_w(3, 1, True)
         mx1(2, 1, 1, acc11)
         s11 = sigmoids(1, 1, acc11)
         hg11 = add_inp(1, 1, s11)

@@ -14,7 +14,7 @@ ALU = mybir.AluOpType
 P = 128
 HALF = 512
 FLOPS = 4 * 2 * 1024 * 1024 * 1024
-PIN = True
+PIN = False
 RAW_BUFS = 7
 
 

@@ -14,7 +14,7 @@ ALU = mybir.AluOpType
 P = 128
 HALF = 512
 FLOPS = 4 * 2 * 1024 * 1024 * 1024
-PIN = False
+PIN = True
 RAW_BUFS = 7
 
 
@@ -35,7 +35,7 @@ def tile_pt_grumb_pb_kernel(
         const = ctx.enter_context(tc.tile_pool(name="const", bufs=1))
         keep = ctx.enter_context(tc.tile_pool(name="keep", bufs=1))
         rawp = ctx.enter_context(tc.tile_pool(name="rawp", bufs=RAW_BUFS))
-        agp = ctx.enter_context(tc.tile_pool(name="agp", bufs=3))
+        agp = ctx.enter_context(tc.tile_pool(name="agp", bufs=4))
         wgp = ctx.enter_context(tc.tile_pool(name="wgp", bufs=4))
         sp = ctx.enter_context(tc.tile_pool(name="sp", bufs=3))
         hgp = ctx.enter_context(tc.tile_pool(name="hgp", bufs=2))
@@ -215,8 +215,14 @@ def tile_pt_grumb_pb_kernel(
                             stop=(G == 1),
                         )
                     o = op.tile([P, HALF], F32, tag="o", name="o%d%d%d" % (h, Go, jj))
-                    nc.scalar.activation(out=o[:], in_=acc[:], func=ACTF.Tanh)
-                    nc.sync.dma_start(out=out_v[Go, jj // 2, jj % 2][:, h * HALF:(h + 1) * HALF], in_=o[:])
+                    pieces = 2 if (h, Go, jj) == (1, 1, 3) else 1
+                    wid = HALF // pieces
+                    for q in range(pieces):
+                        nc.scalar.activation(out=o[:, q * wid:(q + 1) * wid], in_=acc[:, q * wid:(q + 1) * wid], func=ACTF.Tanh)
+                        nc.sync.dma_start(
+                            out=out_v[Go, jj // 2, jj % 2][:, h * HALF + q * wid:h * HALF + (q + 1) * wid],
+                            in_=o[:, q * wid:(q + 1) * wid],
+                        )
 
         for n in range(RAW_BUFS):
             load_next()
@@ -229,10 +235,10 @@ def tile_pt_grumb_pb_kernel(
         mx1(1, 0, 0, acc00)
         prep_act(2, 0)
         prep_w(2, 0)
-        prep_w(0, 1)
+        prep_w(0, 1, True)
         mx1(2, 0, 0, acc00)
         s00 = sigmoids(0, 0, acc00)
-        prep_w(1, 1)
+        prep_w(1, 1, True)
         acc01 = open_accs(0, 1)
         mx1(0, 1, 0, acc01)
         wgs = transpose_w(2, 1)

@@ -35,7 +35,7 @@ def tile_pt_grumb_pb_kernel(
         const = ctx.enter_context(tc.tile_pool(name="const", bufs=1))
         keep = ctx.enter_context(tc.tile_pool(name="keep", bufs=1))
         rawp = ctx.enter_context(tc.tile_pool(name="rawp", bufs=RAW_BUFS))
-        agp = ctx.enter_context(tc.tile_pool(name="agp", bufs=4))
+        agp = ctx.enter_context(tc.tile_pool(name="agp", bufs=3))
         wgp = ctx.enter_context(tc.tile_pool(name="wgp", bufs=4))
         sp = ctx.enter_context(tc.tile_pool(name="sp", bufs=3))
         hgp = ctx.enter_context(tc.tile_pool(name="hgp", bufs=2))
@@ -161,11 +161,31 @@ def tile_pt_grumb_pb_kernel(
             quant_w(w, G, 0, wgs[0])
             quant_w(w, G, 1, wgs[1])
 
+        def transpose_half(w, G, half, share=False):
+            words = raws[("w", w, G)][:].bitcast(F32)
+            wg = wgp.tile([P, 2048], BF16, tag="wg", name="wg%d%d%d" % (w, G, half), align_bytes=64)
+            wgf = wg[:].bitcast(F32).rearrange("p (a g m u) -> p a g m u", a=2, g=2, u=2)
+            banks = []
+            for a2 in range(2):
+                jj = 2 * half + a2
+                tb = psum.tile([P, 4, P], F32, tag="T", name="tb%d%d%d" % (w, G, jj))
+                for b in range(4):
+                    c0 = jj * 512 + b * P
+                    nc.tensor.transpose(tb[:, b, :], words[:, c0:c0 + P], ident[:])
+                banks.append(tb)
+            for a2 in range(2):
+                bank = banks[a2][:].rearrange("p (g u) m -> p g m u", u=2)
+                if share and a2 == 1:
+                    nc.vector.tensor_copy(out=wgf[:, a2], in_=bank)
+                else:
+                    nc.scalar.copy(out=wgf[:, a2], in_=bank)
+            return wg
+
         def open_accs(h, G):
             return [psum.tile([P, HALF], F32, tag="acc", name="acc%d%d%d" % (h, G, jj)) for jj in range(4)]
 
-        def mx1(w, G, h, accs):
-            for jj in range(4):
+        def mx1(w, G, h, accs, tiles=(0, 1, 2, 3)):
+            for jj in tiles:
                 for g in range(2):
                     nc.tensor.matmul_mx(
                         out=accs[jj][:],
@@ -177,10 +197,17 @@ def tile_pt_grumb_pb_kernel(
                         stop=(w == 2 and g == 1),
                     )
 
-        def sigmoids(h, G, accs):
+        def new_s(h, G):
             s = sp.tile([P, 4, HALF], F32, tag="s", name="s%d%d" % (h, G))
-            for jj in range(4):
+            return s
+
+        def sig(s, accs, tiles):
+            for jj in tiles:
                 nc.scalar.activation(out=s[:, jj, :], in_=accs[jj][:], func=ACTF.Sigmoid)
+
+        def sigmoids(h, G, accs):
+            s = new_s(h, G)
+            sig(s, accs, (0, 1, 2, 3))
             return s
 
         def add_inp(h, G, s):
@@ -215,15 +242,11 @@ def tile_pt_grumb_pb_kernel(
                             stop=(G == 1),
                         )
                     o = op.tile([P, HALF], F32, tag="o", name="o%d%d%d" % (h, Go, jj))
-                    pieces = 2 if (h, Go, jj) == (1, 1, 3) else 1
-                    wid = HALF // pieces
-                    for q in range(pieces):
-                        nc.scalar.activation(out=o[:, q * wid:(q + 1) * wid], in_=acc[:, q * wid:(q + 1) * wid], func=ACTF.Tanh)
-                        nc.sync.dma_start(
-                            out=out_v[Go, jj // 2, jj % 2][:, h * HALF + q * wid:h * HALF + (q + 1) * wid],
-                            in_=o[:, q * wid:(q + 1) * wid],
-                        )
+                    nc.scalar.activation(out=o[:], in_=acc[:], func=ACTF.Tanh)
+                    nc.sync.dma_start(out=out_v[Go, jj // 2, jj % 2][:, h * HALF:(h + 1) * HALF], in_=o[:])
 
+        LO = (0, 1)
+        HI = (2, 3)
         for n in range(RAW_BUFS):
             load_next()
         acc00 = open_accs(0, 0)
@@ -235,21 +258,36 @@ def tile_pt_grumb_pb_kernel(
         mx1(1, 0, 0, acc00)
         prep_act(2, 0)
         prep_w(2, 0)
-        prep_w(0, 1, True)
-        mx1(2, 0, 0, acc00)
-        s00 = sigmoids(0, 0, acc00)
-        prep_w(1, 1, True)
+        wa = transpose_half(0, 1, 0)
+        quant_w(0, 1, 0, wa)
+        mx1(2, 0, 0, acc00, LO)
+        s00 = new_s(0, 0)
+        sig(s00, acc00, LO)
+        wb = transpose_half(0, 1, 1)
+        load_next()
+        quant_w(0, 1, 1, wb)
+        mx1(2, 0, 0, acc00, HI)
+        sig(s00, acc00, HI)
         acc01 = open_accs(0, 1)
-        mx1(0, 1, 0, acc01)
-        wgs = transpose_w(2, 1)
+        wa = transpose_half(1, 1, 0)
+        quant_w(1, 1, 0, wa)
+        mx1(0, 1, 0, acc01, LO)
+        wb = transpose_half(1, 1, 1)
+        load_next()
+        quant_w(1, 1, 1, wb)
+        mx1(0, 1, 0, acc01, HI)
+        wa = transpose_half(2, 1, 0)
         ag0 = regroup(0, 1, 0)
-        quant_w(2, 1, 0, wgs[0])
+        quant_w(2, 1, 0, wa)
+        mx1(1, 1, 0, acc01, LO)
+        wb = transpose_half(2, 1, 1)
+        load_next()
         ag1 = regroup(0, 1, 1)
-        quant_w(2, 1, 1, wgs[1])
+        quant_w(2, 1, 1, wb)
+        mx1(1, 1, 0, acc01, HI)
         quant_act(0, 1, 0, ag0)
         quant_act(0, 1, 1, ag1)
         load_next()
-        mx1(1, 1, 0, acc01)
         mx1(2, 1, 0, acc01)
         s01 = sigmoids(0, 1, acc01)
         prep_act(1, 1)
@@ -268,14 +306,22 @@ def tile_pt_grumb_pb_kernel(
         mx1(2, 0, 1, acc10)
         s10 = sigmoids(1, 0, acc10)
         acc11 = open_accs(1, 1)
-        mx1(0, 1, 1, acc11)
-        wgs0 = transpose_w(3, 0, True)
+        mx1(0, 1, 1, acc11, LO)
+        wa = transpose_half(3, 0, 0, True)
+        mx1(0, 1, 1, acc11, HI)
+        wb = transpose_half(3, 0, 1, True)
+        load_next()
         hg10 = add_inp(1, 0, s10)
-        quant_w(3, 0, 0, wgs0[0])
-        quant_w(3, 0, 1, wgs0[1])
+        quant_w(3, 0, 0, wa)
+        quant_w(3, 0, 1, wb)
         quant_h(1, 0, hg10)
-        mx1(1, 1, 1, acc11)
-        prep_w(3, 1, True)
+        mx1(1, 1, 1, acc11, LO)
+        wa = transpose_half(3, 1, 0, True)
+        quant_w(3, 1, 0, wa)
+        mx1(1, 1, 1, acc11, HI)
+        wb = transpose_half(3, 1, 1, True)
+        load_next()
+        quant_w(3, 1, 1, wb)
         mx1(2, 1, 1, acc11)
         s11 = sigmoids(1, 1, acc11)
         hg11 = add_inp(1, 1, s11)

@@ -10,13 +10,12 @@ U8 = mybir.dt.uint8
 FP8X4 = mybir.dt.float8_e4m3fn_x4
 ACTF = mybir.ActivationFunctionType
 ALU = mybir.AluOpType
-
 P = 128
 HALF = 512
 FLOPS = 4 * 2 * 1024 * 1024 * 1024
-PIN = True
-RAW_BUFS = 7
-
+LO = (0, 1)
+HI = (2, 3)
+ALL = (0, 1, 2, 3)
 
 def tile_pt_grumb_pb_kernel(
     tc, x, out0, mem0, inp_out, w_readgate, w_rec_readgate, w_mem_readgate, w_hid_out, out
@@ -30,23 +29,30 @@ def tile_pt_grumb_pb_kernel(
     out_v = out.rearrange("(G U p E) c -> G U E p c", G=2, U=2, E=2)
 
     with ExitStack() as ctx:
-        if PIN:
-            ctx.enter_context(tc.manual_schedule())
+        ctx.enter_context(tc.manual_schedule())
         const = ctx.enter_context(tc.tile_pool(name="const", bufs=1))
         keep = ctx.enter_context(tc.tile_pool(name="keep", bufs=1))
-        rawp = ctx.enter_context(tc.tile_pool(name="rawp", bufs=RAW_BUFS))
+        rawp = ctx.enter_context(tc.tile_pool(name="rawp", bufs=14))
         agp = ctx.enter_context(tc.tile_pool(name="agp", bufs=3))
         wgp = ctx.enter_context(tc.tile_pool(name="wgp", bufs=4))
         sp = ctx.enter_context(tc.tile_pool(name="sp", bufs=3))
         hgp = ctx.enter_context(tc.tile_pool(name="hgp", bufs=2))
         op = ctx.enter_context(tc.tile_pool(name="op", bufs=6))
-        psum = ctx.enter_context(tc.psum_pool(name="psum", bufs=4))
+        psa = ctx.enter_context(tc.psum_pool(name="psa", bufs=4))
+        pst = ctx.enter_context(tc.psum_pool(name="pst", bufs=4))
 
         ident = const.tile([P, P], F32, name="ident")
         make_identity(nc, ident[:])
         warm = const.tile([P, 8], F32, name="warm")
         nc.vector.memset(warm[:], 0.0)
         nc.scalar.activation(out=warm[:], in_=warm[:], func=ACTF.Sigmoid)
+        WARM = 0
+        if WARM:
+            dum = const.tile([P, HALF], BF16, name="dum")
+            nc.gpsimd.memset(dum[:], 0.0)
+            dps = psa.tile([P, HALF], F32, tag="acc", name="dps")
+            for n in range(WARM):
+                nc.tensor.matmul(out=dps[:], lhsT=dum[:, 0:P], rhs=dum[:], start=True, stop=True)
 
         inp = keep.tile([P, 2, 4, 1024], BF16, name="inp")
         a_codes = {}
@@ -67,264 +73,282 @@ def tile_pt_grumb_pb_kernel(
                 w_codes[(w, G)] = keep.tile([P, 4, 2, P], U32, name="wc%d%d" % (w, G), align_bytes=64)
                 w_scales[(w, G)] = keep.tile([P, 4, 2, P], U8, name="ws%d%d" % (w, G), align_bytes=64)
 
-        loads = [
-            ("a", 0, 0), ("w", 0, 0), ("a", 1, 0), ("w", 1, 0), ("a", 2, 0), ("w", 2, 0),
-            ("w", 0, 1), ("w", 1, 1), ("w", 2, 1), ("a", 0, 1), ("a", 1, 1), ("a", 2, 1),
-            ("w", 3, 0), ("w", 3, 1),
-        ]
+        loads = [('w', 0, 0, 0), ('w', 0, 0, 1), ('a', 0, 0, 0), ('a', 0, 0, 1), ('w', 1, 0, 0), ('w', 1, 0, 1), ('a', 1, 0, 0), ('a', 1, 0, 1), ('w', 2, 0, 0), ('w', 2, 0, 1), ('a', 2, 0, 0), ('a', 2, 0, 1), ('w', 0, 1, 0), ('w', 0, 1, 1), ('w', 1, 1, 0), ('w', 1, 1, 1), ('w', 2, 1, 0), ('w', 2, 1, 1), ('a', 0, 1, 0), ('a', 0, 1, 1), ('a', 1, 1, 0), ('a', 1, 1, 1), ('a', 2, 1, 0), ('a', 2, 1, 1), ('i', 2, 0), ('i', 2, 1), ('w', 3, 0, 0), ('w', 3, 0, 1), ('w', 3, 1, 0), ('w', 3, 1, 1)]
         raws = {}
         nxt = [0]
 
-        def load_next():
-            if nxt[0] >= len(loads):
-                return
-            kind, i, j = loads[nxt[0]]
-            nxt[0] += 1
-            raw = rawp.tile([P, 4096], BF16, tag="raw", name="raw_%s%d%d" % (kind, i, j))
-            raws[(kind, i, j)] = raw
-            if kind == "a":
-                for g in range(2):
-                    for u in range(2):
-                        o = (4 * g + 2 * u) * HALF
+        order = []
+        used = set()
+
+        def pump():
+            while nxt[0] < len(loads):
+                key = loads[nxt[0]]
+                if key[0] != "i" and len(order) >= 14 and order[-14] not in used:
+                    return
+                nxt[0] += 1
+                if key[0] == "i":
+                    i, G = key[1], key[2]
+                    for U in range(2):
                         nc.sync.dma_start(
-                            out=raw[:, o:o + 2 * HALF].rearrange("p (e c) -> p e c", e=2),
-                            in_=act_v[i][g, u][:, :, j * HALF:(j + 1) * HALF],
+                            out=inp[:, G, 2 * U:2 * U + 2, :].rearrange("p t c -> p (t c)"),
+                            in_=inp_v[G, U],
                         )
-                if (i, j) == (2, 1):
-                    for G in range(2):
-                        for U in range(2):
-                            nc.sync.dma_start(
-                                out=inp[:, G, 2 * U:2 * U + 2, :].rearrange("p t c -> p (t c)"),
-                                in_=inp_v[G, U],
-                            )
-            else:
-                for U in range(2):
-                    nc.sync.dma_start(out=raw[:, U * 2048:(U + 1) * 2048], in_=w_v[i][j, U])
+                    continue
+                order.append(key)
+                raw = rawp.tile([P, 2048], BF16, tag="raw", name="raw_%s%d%d%d" % key)
+                raws[key] = raw
+                kind, i, j, s = key
+                if kind == "a":
+                    for u in range(2):
+                        nc.sync.dma_start(
+                            out=raw[:, u * 2 * HALF:(u + 1) * 2 * HALF].rearrange("p (e c) -> p e c", e=2),
+                            in_=act_v[i][s, u][:, :, j * HALF:(j + 1) * HALF],
+                        )
+                else:
+                    nc.sync.dma_start(out=raw[:], in_=w_v[i][j, s])
 
-        def regroup(a, h, g, on_scalar=False):
-            raw = raws[("a", a, h)]
+        ags = {}
+
+        def R(a, h, g, eng="V"):
             ag = agp.tile([P, 2048], BF16, tag="ag", name="ag%d%d%d" % (a, h, g), align_bytes=64)
-            dst = ag[:].rearrange("p (c i t) -> p c t i", i=4, t=4)
-            src = raw[:, g * 2048:(g + 1) * 2048].rearrange("p (t c i) -> p c t i", t=4, i=4)
-            if on_scalar:
-                nc.scalar.copy(out=dst, in_=src)
-            else:
-                nc.vector.tensor_copy(out=dst, in_=src)
-            return ag
+            ags[(a, h, g)] = ag
+            raw = raws[("a", a, h, g)]
+            ends = {"V": ((0, HALF, "V"),), "S": ((0, HALF, "S"),)}
+            for c0, c1, e in ends.get(eng) or ((0, int(eng[1:]), "V"), (int(eng[1:]), HALF, "S")):
+                dst = ag[:, 4 * c0:4 * c1].rearrange("p (c i t) -> p c t i", i=4, t=4)
+                src = raw[:].rearrange("p (t c) -> p t c", t=4)[:, :, c0:c1].rearrange("p t (c i) -> p c t i", i=4)
+                if e == "S":
+                    nc.scalar.copy(out=dst, in_=src)
+                else:
+                    nc.vector.tensor_copy(out=dst, in_=src)
+            used.add(("a", a, h, g))
+            pump()
 
-        def quant_act(a, h, g, ag):
+        def A(a, h, g):
             nc.vector.quantize_mx(
                 out=a_codes[(a, h)][:, g, :].bitcast(FP8X4),
                 scales=a_scales[(a, h)][:, g, :],
-                in_=ag[:],
+                in_=ags[(a, h, g)][:],
             )
 
-        def prep_act(a, h):
-            ag0 = regroup(a, h, 0)
-            ag1 = regroup(a, h, 1)
-            quant_act(a, h, 0, ag0)
-            quant_act(a, h, 1, ag1)
-            load_next()
+        tbs = {}
 
-        def transpose_w(w, G, share=False):
-            words = raws[("w", w, G)][:].bitcast(F32)
-            banks = []
-            for jj in range(4):
-                tb = psum.tile([P, 4, P], F32, tag="T", name="tb%d%d%d" % (w, G, jj))
+        def T(w, G, U):
+            words = raws[("w", w, G, U)][:].bitcast(F32)
+            for E in range(2):
+                tb = pst.tile([P, 4, P], F32, tag="T", name="tb%d%d%d%d" % (w, G, U, E))
                 for b in range(4):
-                    c0 = jj * 512 + b * P
+                    c0 = E * 512 + b * P
                     nc.tensor.transpose(tb[:, b, :], words[:, c0:c0 + P], ident[:])
-                banks.append(tb)
-            load_next()
-            wgs = []
-            for half in range(2):
-                wg = wgp.tile([P, 2048], BF16, tag="wg", name="wg%d%d%d" % (w, G, half), align_bytes=64)
-                wgf = wg[:].bitcast(F32).rearrange("p (a g m u) -> p a g m u", a=2, g=2, u=2)
-                for a2 in range(2):
-                    bank = banks[2 * half + a2][:].rearrange("p (g u) m -> p g m u", u=2)
-                    if share and a2 == 1:
-                        nc.vector.tensor_copy(out=wgf[:, a2], in_=bank)
-                    else:
-                        nc.scalar.copy(out=wgf[:, a2], in_=bank)
-                wgs.append(wg)
-            return wgs
+                tbs[(w, G, U, E)] = tb
+            used.add(("w", w, G, U))
+            pump()
 
-        def quant_w(w, G, half, wg):
-            nc.vector.quantize_mx(
-                out=w_codes[(w, G)][:, 2 * half:2 * half + 2].rearrange("p a g m -> p (a g m)").bitcast(FP8X4),
-                scales=w_scales[(w, G)][:, 2 * half:2 * half + 2].rearrange("p a g m -> p (a g m)"),
-                in_=wg[:],
-            )
+        wgs = {}
 
-        def prep_w(w, G, share=False):
-            wgs = transpose_w(w, G, share)
-            quant_w(w, G, 0, wgs[0])
-            quant_w(w, G, 1, wgs[1])
-
-        def transpose_half(w, G, half, share=False):
-            words = raws[("w", w, G)][:].bitcast(F32)
-            wg = wgp.tile([P, 2048], BF16, tag="wg", name="wg%d%d%d" % (w, G, half), align_bytes=64)
+        def C(w, G, U, eng="SS"):
+            wg = wgp.tile([P, 2048], BF16, tag="wg", name="wg%d%d%d" % (w, G, U), align_bytes=64)
+            wgs[(w, G, U)] = wg
             wgf = wg[:].bitcast(F32).rearrange("p (a g m u) -> p a g m u", a=2, g=2, u=2)
-            banks = []
-            for a2 in range(2):
-                jj = 2 * half + a2
-                tb = psum.tile([P, 4, P], F32, tag="T", name="tb%d%d%d" % (w, G, jj))
-                for b in range(4):
-                    c0 = jj * 512 + b * P
-                    nc.tensor.transpose(tb[:, b, :], words[:, c0:c0 + P], ident[:])
-                banks.append(tb)
-            for a2 in range(2):
-                bank = banks[a2][:].rearrange("p (g u) m -> p g m u", u=2)
-                if share and a2 == 1:
-                    nc.vector.tensor_copy(out=wgf[:, a2], in_=bank)
+            for E in range(2):
+                bank = tbs[(w, G, U, E)][:].rearrange("p (g u) m -> p g m u", u=2)
+                if eng[E] == "V":
+                    nc.vector.tensor_copy(out=wgf[:, E], in_=bank)
                 else:
-                    nc.scalar.copy(out=wgf[:, a2], in_=bank)
-            return wg
+                    nc.scalar.copy(out=wgf[:, E], in_=bank)
 
-        def open_accs(h, G):
-            return [psum.tile([P, HALF], F32, tag="acc", name="acc%d%d%d" % (h, G, jj)) for jj in range(4)]
+        def Q(w, G, U):
+            nc.vector.quantize_mx(
+                out=w_codes[(w, G)][:, 2 * U:2 * U + 2].rearrange("p a g m -> p (a g m)").bitcast(FP8X4),
+                scales=w_scales[(w, G)][:, 2 * U:2 * U + 2].rearrange("p a g m -> p (a g m)"),
+                in_=wgs[(w, G, U)][:],
+            )
 
-        def mx1(w, G, h, accs, tiles=(0, 1, 2, 3)):
+        accs = {}
+
+        def X(w, G, h, tiles=ALL, gs=(0, 1), gouter=False):
+            order = [(jj, g) for g in gs for jj in tiles] if gouter else [(jj, g) for jj in tiles for g in gs]
+            for jj, g in order:
+                k = (h, G, jj)
+                if w == 0 and g == 0:
+                    accs[k] = psa.tile([P, HALF], F32, tag="acc", name="acc%d%d%d" % k)
+                nc.tensor.matmul_mx(
+                    out=accs[k][:],
+                    lhsT=w_codes[(w, G)][:, jj, g, :].bitcast(FP8X4),
+                    lhsT_scale=w_scales[(w, G)][:, jj, g, :],
+                    rhs=a_codes[(w, h)][:, g, :].bitcast(FP8X4),
+                    rhs_scale=a_scales[(w, h)][:, g, :],
+                    start=(w == 0 and g == 0),
+                    stop=(w == 2 and g == 1),
+                )
+
+        ss = {}
+
+        def S(h, G, tiles=ALL):
+            if (h, G) not in ss:
+                s = sp.tile([P, 4, HALF], F32, tag="s", name="s%d%d" % (h, G))
+                ss[(h, G)] = s
             for jj in tiles:
-                for g in range(2):
-                    nc.tensor.matmul_mx(
-                        out=accs[jj][:],
-                        lhsT=w_codes[(w, G)][:, jj, g, :].bitcast(FP8X4),
-                        lhsT_scale=w_scales[(w, G)][:, jj, g, :],
-                        rhs=a_codes[(w, h)][:, g, :].bitcast(FP8X4),
-                        rhs_scale=a_scales[(w, h)][:, g, :],
-                        start=(w == 0 and g == 0),
-                        stop=(w == 2 and g == 1),
-                    )
+                nc.scalar.activation(out=ss[(h, G)][:, jj, :], in_=accs[(h, G, jj)][:], func=ACTF.Sigmoid)
 
-        def new_s(h, G):
-            s = sp.tile([P, 4, HALF], F32, tag="s", name="s%d%d" % (h, G))
-            return s
+        hgs = {}
 
-        def sig(s, accs, tiles):
-            for jj in tiles:
-                nc.scalar.activation(out=s[:, jj, :], in_=accs[jj][:], func=ACTF.Sigmoid)
-
-        def sigmoids(h, G, accs):
-            s = new_s(h, G)
-            sig(s, accs, (0, 1, 2, 3))
-            return s
-
-        def add_inp(h, G, s):
-            hg = hgp.tile([P, HALF, 4], BF16, tag="hg", name="hg%d%d" % (h, G), align_bytes=64)
+        def H(h, G, c0=0, c1=HALF):
+            if (h, G) not in hgs:
+                hg = hgp.tile([P, HALF, 4], BF16, tag="hg", name="hg%d%d" % (h, G), align_bytes=64)
+                hgs[(h, G)] = hg
             nc.vector.tensor_tensor(
-                out=hg[:].rearrange("p (c i) t -> p c t i", i=4),
-                in0=s[:].rearrange("p t (c i) -> p c t i", i=4),
-                in1=inp[:, G, :, h * HALF:(h + 1) * HALF].rearrange("p t (c i) -> p c t i", i=4),
+                out=hgs[(h, G)][:, c0:c1].rearrange("p (c i) t -> p c t i", i=4),
+                in0=ss[(h, G)][:, :, c0:c1].rearrange("p t (c i) -> p c t i", i=4),
+                in1=inp[:, G, :, h * HALF + c0:h * HALF + c1].rearrange("p t (c i) -> p c t i", i=4),
                 op=ALU.add,
             )
-            return hg
 
-        def quant_h(h, G, hg):
+        def K(h, G, c0=0, c1=HALF):
             nc.vector.quantize_mx(
-                out=h_codes[(h, G)][:].bitcast(FP8X4),
-                scales=h_scales[(h, G)][:],
-                in_=hg[:].rearrange("p c t -> p (c t)"),
+                out=h_codes[(h, G)][:, c0:c1].bitcast(FP8X4),
+                scales=h_scales[(h, G)][:, c0:c1],
+                in_=hgs[(h, G)][:, c0:c1].rearrange("p c t -> p (c t)"),
             )
 
-        def stage2(h):
-            for Go in range(2):
-                for jj in range(4):
-                    acc = psum.tile([P, HALF], F32, tag="acc", name="o_acc%d%d%d" % (h, Go, jj))
-                    for G in range(2):
-                        nc.tensor.matmul_mx(
-                            out=acc[:],
-                            lhsT=w_codes[(3, Go)][:, jj, G, :].bitcast(FP8X4),
-                            lhsT_scale=w_scales[(3, Go)][:, jj, G, :],
-                            rhs=h_codes[(h, G)][:].bitcast(FP8X4),
-                            rhs_scale=h_scales[(h, G)][:],
-                            start=(G == 0),
-                            stop=(G == 1),
-                        )
-                    o = op.tile([P, HALF], F32, tag="o", name="o%d%d%d" % (h, Go, jj))
-                    nc.scalar.activation(out=o[:], in_=acc[:], func=ACTF.Tanh)
-                    nc.sync.dma_start(out=out_v[Go, jj // 2, jj % 2][:, h * HALF:(h + 1) * HALF], in_=o[:])
+        oacc = {}
 
-        LO = (0, 1)
-        HI = (2, 3)
-        for n in range(RAW_BUFS):
-            load_next()
-        acc00 = open_accs(0, 0)
-        prep_act(0, 0)
-        prep_w(0, 0)
-        mx1(0, 0, 0, acc00)
-        prep_act(1, 0)
-        prep_w(1, 0)
-        mx1(1, 0, 0, acc00)
-        prep_act(2, 0)
-        prep_w(2, 0)
-        wa = transpose_half(0, 1, 0)
-        quant_w(0, 1, 0, wa)
-        mx1(2, 0, 0, acc00, LO)
-        s00 = new_s(0, 0)
-        sig(s00, acc00, LO)
-        wb = transpose_half(0, 1, 1)
-        load_next()
-        quant_w(0, 1, 1, wb)
-        mx1(2, 0, 0, acc00, HI)
-        sig(s00, acc00, HI)
-        acc01 = open_accs(0, 1)
-        wa = transpose_half(1, 1, 0)
-        quant_w(1, 1, 0, wa)
-        mx1(0, 1, 0, acc01, LO)
-        wb = transpose_half(1, 1, 1)
-        load_next()
-        quant_w(1, 1, 1, wb)
-        mx1(0, 1, 0, acc01, HI)
-        wa = transpose_half(2, 1, 0)
-        ag0 = regroup(0, 1, 0)
-        quant_w(2, 1, 0, wa)
-        mx1(1, 1, 0, acc01, LO)
-        wb = transpose_half(2, 1, 1)
-        load_next()
-        ag1 = regroup(0, 1, 1)
-        quant_w(2, 1, 1, wb)
-        mx1(1, 1, 0, acc01, HI)
-        quant_act(0, 1, 0, ag0)
-        quant_act(0, 1, 1, ag1)
-        load_next()
-        mx1(2, 1, 0, acc01)
-        s01 = sigmoids(0, 1, acc01)
-        prep_act(1, 1)
-        acc10 = open_accs(1, 0)
-        mx1(0, 0, 1, acc10)
-        ag0 = regroup(2, 1, 0)
-        ag1 = regroup(2, 1, 1, True)
-        quant_act(2, 1, 0, ag0)
-        quant_act(2, 1, 1, ag1)
-        load_next()
-        hg00 = add_inp(0, 0, s00)
-        hg01 = add_inp(0, 1, s01)
-        quant_h(0, 0, hg00)
-        quant_h(0, 1, hg01)
-        mx1(1, 0, 1, acc10)
-        mx1(2, 0, 1, acc10)
-        s10 = sigmoids(1, 0, acc10)
-        acc11 = open_accs(1, 1)
-        mx1(0, 1, 1, acc11, LO)
-        wa = transpose_half(3, 0, 0, True)
-        mx1(0, 1, 1, acc11, HI)
-        wb = transpose_half(3, 0, 1, True)
-        load_next()
-        hg10 = add_inp(1, 0, s10)
-        quant_w(3, 0, 0, wa)
-        quant_w(3, 0, 1, wb)
-        quant_h(1, 0, hg10)
-        mx1(1, 1, 1, acc11, LO)
-        wa = transpose_half(3, 1, 0, True)
-        quant_w(3, 1, 0, wa)
-        mx1(1, 1, 1, acc11, HI)
-        wb = transpose_half(3, 1, 1, True)
-        load_next()
-        quant_w(3, 1, 1, wb)
-        mx1(2, 1, 1, acc11)
-        s11 = sigmoids(1, 1, acc11)
-        hg11 = add_inp(1, 1, s11)
-        quant_h(1, 1, hg11)
-        stage2(0)
-        stage2(1)
+        def O(h, Go, jj, gs=(0, 1)):
+            k = (h, Go, jj)
+            for G in gs:
+                if G == 0:
+                    oacc[k] = psa.tile([P, HALF], F32, tag="acc", name="o_acc%d%d%d" % k)
+                nc.tensor.matmul_mx(
+                    out=oacc[k][:],
+                    lhsT=w_codes[(3, Go)][:, jj, G, :].bitcast(FP8X4),
+                    lhsT_scale=w_scales[(3, Go)][:, jj, G, :],
+                    rhs=h_codes[(h, G)][:].bitcast(FP8X4),
+                    rhs_scale=h_scales[(h, G)][:],
+                    start=(G == 0),
+                    stop=(G == 1),
+                )
+
+        def Y(h, Go, jj):
+            o = op.tile([P, HALF], F32, tag="o", name="o%d%d%d" % (h, Go, jj))
+            nc.scalar.activation(out=o[:], in_=oacc[(h, Go, jj)][:], func=ACTF.Tanh)
+            nc.sync.dma_start(out=out_v[Go, jj // 2, jj % 2][:, h * HALF:(h + 1) * HALF], in_=o[:])
+
+        def OY(h, Go, jj):
+            O(h, Go, jj)
+            Y(h, Go, jj)
+
+        pump()
+        T(0,0,0)
+        C(0,0,0)
+        T(0,0,1)
+        R(0,0,0,"x352")
+        C(0,0,1)
+        Q(0,0,0)
+        R(0,0,1,"x352")
+        A(0,0,0)
+        Q(0,0,1)
+        A(0,0,1)
+        T(1,0,0)
+        C(1,0,0)
+        T(1,0,1)
+        C(1,0,1)
+        X(0,0,0,ALL,(0,1))
+        R(1,0,0,"x352")
+        Q(1,0,0)
+        R(1,0,1,"x352")
+        A(1,0,0)
+        Q(1,0,1)
+        A(1,0,1)
+        T(2,0,0)
+        C(2,0,0)
+        T(2,0,1)
+        C(2,0,1)
+        X(1,0,0,ALL,(0,1))
+        R(2,0,0,"x352")
+        Q(2,0,0)
+        R(2,0,1,"x352")
+        A(2,0,0)
+        Q(2,0,1)
+        A(2,0,1)
+        T(0,1,0)
+        C(0,1,0)
+        T(0,1,1)
+        X(2,0,0,LO)
+        S(0,0,LO)
+        C(0,1,1)
+        Q(0,1,0)
+        Q(0,1,1)
+        X(2,0,0,HI)
+        S(0,0,HI)
+        T(1,1,0)
+        T(1,1,1)
+        C(1,1,0)
+        C(1,1,1)
+        X(0,1,0)
+        Q(1,1,0)
+        Q(1,1,1)
+        T(2,1,0)
+        T(2,1,1)
+        C(2,1,0)
+        C(2,1,1)
+        R(0,1,0,"x384")
+        R(0,1,1,"x384")
+        X(1,1,0)
+        Q(2,1,0)
+        Q(2,1,1)
+        A(0,1,0)
+        A(0,1,1)
+        R(1,1,0,"x384")
+        X(2,1,0)
+        S(0,1)
+        R(1,1,1,"x384")
+        A(1,1,0)
+        X(0,0,1)
+        R(2,1,0,"x384")
+        A(1,1,1)
+        R(2,1,1,"x384")
+        A(2,1,0)
+        X(1,0,1)
+        A(2,1,1)
+        H(0,0)
+        H(0,1)
+        K(0,0)
+        K(0,1)
+        X(2,0,1)
+        S(1,0)
+        T(3,0,0)
+        C(3,0,0,"SS")
+        T(3,0,1)
+        C(3,0,1,"SS")
+        X(0,1,1)
+        H(1,0)
+        Q(3,0,0)
+        Q(3,0,1)
+        K(1,0)
+        T(3,1,0)
+        C(3,1,0,"SS")
+        T(3,1,1)
+        C(3,1,1,"SS")
+        X(1,1,1)
+        Q(3,1,0)
+        Q(3,1,1)
+        X(2,1,1)
+        S(1,1)
+        H(1,1)
+        K(1,1)
+        OY(0,0,0)
+        OY(0,0,1)
+        OY(0,0,2)
+        OY(0,0,3)
+        OY(0,1,0)
+        OY(0,1,1)
+        OY(0,1,2)
+        OY(0,1,3)
+        OY(1,0,0)
+        OY(1,0,1)
+        OY(1,0,2)
+        OY(1,0,3)
+        OY(1,1,0)
+        OY(1,1,1)
+        OY(1,1,2)
+        OY(1,1,3)

@@ -46,13 +46,6 @@ def tile_pt_grumb_pb_kernel(
         warm = const.tile([P, 8], F32, name="warm")
         nc.vector.memset(warm[:], 0.0)
         nc.scalar.activation(out=warm[:], in_=warm[:], func=ACTF.Sigmoid)
-        WARM = 0
-        if WARM:
-            dum = const.tile([P, HALF], BF16, name="dum")
-            nc.gpsimd.memset(dum[:], 0.0)
-            dps = psa.tile([P, HALF], F32, tag="acc", name="dps")
-            for n in range(WARM):
-                nc.tensor.matmul(out=dps[:], lhsT=dum[:, 0:P], rhs=dum[:], start=True, stop=True)
 
         inp = keep.tile([P, 2, 4, 1024], BF16, name="inp")
         a_codes = {}
@@ -73,7 +66,7 @@ def tile_pt_grumb_pb_kernel(
                 w_codes[(w, G)] = keep.tile([P, 4, 2, P], U32, name="wc%d%d" % (w, G), align_bytes=64)
                 w_scales[(w, G)] = keep.tile([P, 4, 2, P], U8, name="ws%d%d" % (w, G), align_bytes=64)
 
-        loads = [('w', 0, 0, 0), ('w', 0, 0, 1), ('a', 0, 0, 0), ('a', 0, 0, 1), ('w', 1, 0, 0), ('w', 1, 0, 1), ('a', 1, 0, 0), ('a', 1, 0, 1), ('w', 2, 0, 0), ('w', 2, 0, 1), ('a', 2, 0, 0), ('a', 2, 0, 1), ('w', 0, 1, 0), ('w', 0, 1, 1), ('w', 1, 1, 0), ('w', 1, 1, 1), ('w', 2, 1, 0), ('w', 2, 1, 1), ('a', 0, 1, 0), ('a', 0, 1, 1), ('a', 1, 1, 0), ('a', 1, 1, 1), ('a', 2, 1, 0), ('a', 2, 1, 1), ('i', 2, 0), ('i', 2, 1), ('w', 3, 0, 0), ('w', 3, 0, 1), ('w', 3, 1, 0), ('w', 3, 1, 1)]
+        loads = [('w', 0, 0, 0), ('w', 0, 0, 1), ('a', 0, 0, 0), ('a', 0, 0, 1), ('w', 1, 0, 0), ('w', 1, 0, 1), ('a', 1, 0, 0), ('a', 1, 0, 1), ('w', 2, 0, 0), ('w', 2, 0, 1), ('a', 2, 0, 0), ('a', 2, 0, 1), ('w', 0, 1, 0), ('w', 0, 1, 1), ('w', 1, 1, 0), ('w', 1, 1, 1), ('a', 0, 1, 0), ('a', 0, 1, 1), ('w', 2, 1, 0), ('w', 2, 1, 1), ('a', 1, 1, 0), ('a', 1, 1, 1), ('a', 2, 1, 0), ('a', 2, 1, 1), ('i', 2, 0), ('i', 2, 1), ('w', 3, 0, 0), ('w', 3, 0, 1), ('w', 3, 1, 0), ('w', 3, 1, 1)]
         raws = {}
         nxt = [0]
 
@@ -285,28 +278,28 @@ def tile_pt_grumb_pb_kernel(
         C(1,1,0)
         C(1,1,1)
         X(0,1,0)
+        R(0,1,0,"V")
         Q(1,1,0)
         Q(1,1,1)
+        R(0,1,1,"V")
         T(2,1,0)
         T(2,1,1)
         C(2,1,0)
         C(2,1,1)
-        R(0,1,0,"x384")
-        R(0,1,1,"x384")
+        A(0,1,0)
         X(1,1,0)
         Q(2,1,0)
         Q(2,1,1)
-        A(0,1,0)
         A(0,1,1)
-        R(1,1,0,"x384")
+        R(1,1,0,"x320")
+        R(1,1,1,"x320")
         X(2,1,0)
         S(0,1)
-        R(1,1,1,"x384")
         A(1,1,0)
-        X(0,0,1)
-        R(2,1,0,"x384")
         A(1,1,1)
-        R(2,1,1,"x384")
+        X(0,0,1)
+        R(2,1,0,"x320")
+        R(2,1,1,"x320")
         A(2,1,0)
         X(1,0,1)
         A(2,1,1)

@@ -47,6 +47,8 @@ def tile_pt_grumb_pb_kernel(
         nc.vector.memset(warm[:], 0.0)
         nc.scalar.activation(out=warm[:], in_=warm[:], func=ACTF.Sigmoid)
 
+        dum = const.tile([P, HALF], BF16, name="dum")
+        nc.vector.memset(dum[:], 0.0)
         inp = keep.tile([P, 2, 4, 1024], BF16, name="inp")
         a_codes = {}
         a_scales = {}
@@ -126,10 +128,13 @@ def tile_pt_grumb_pb_kernel(
 
         tbs = {}
 
-        def T(w, G, U):
+        def T(w, G, U, pre=0):
             words = raws[("w", w, G, U)][:].bitcast(F32)
             for E in range(2):
                 tb = pst.tile([P, 4, P], F32, tag="T", name="tb%d%d%d%d" % (w, G, U, E))
+                if E == 0:
+                    for n in range(pre):
+                        nc.tensor.matmul(out=tb[:].rearrange("p a m -> p (a m)"), lhsT=dum[:, 0:P], rhs=dum[:], start=True, stop=True)
                 for b in range(4):
                     c0 = E * 512 + b * P
                     nc.tensor.transpose(tb[:, b, :], words[:, c0:c0 + P], ident[:])
@@ -231,7 +236,7 @@ def tile_pt_grumb_pb_kernel(
             Y(h, Go, jj)
 
         pump()
-        T(0,0,0)
+        T(0,0,0,6)
         C(0,0,0)
         T(0,0,1)
         R(0,0,0,"x352")
@@ -241,7 +246,7 @@ def tile_pt_grumb_pb_kernel(
         A(0,0,0)
         Q(0,0,1)
         A(0,0,1)
-        T(1,0,0)
+        T(1,0,0,4)
         C(1,0,0)
         T(1,0,1)
         C(1,0,1)
@@ -252,7 +257,7 @@ def tile_pt_grumb_pb_kernel(
         A(1,0,0)
         Q(1,0,1)
         A(1,0,1)
-        T(2,0,0)
+        T(2,0,0,0)
         C(2,0,0)
         T(2,0,1)
         C(2,0,1)

@@ -56,17 +56,17 @@ def tile_pt_grumb_pb_kernel(
         h_scales = {}
         for h in range(2):
             for a in range(3):
-                a_codes[(a, h)] = keep.tile([P, 2, HALF], U32, name="ac%d%d" % (a, h), align_bytes=64)
-                a_scales[(a, h)] = keep.tile([P, 2, HALF], U8, name="as%d%d" % (a, h), align_bytes=64)
+                a_codes[(a, h)] = keep.tile([P, 2, HALF], U32, name="ac%d%d" % (a, h), align_bytes=256)
+                a_scales[(a, h)] = keep.tile([P, 2, HALF], U8, name="as%d%d" % (a, h), align_bytes=256)
             for G in range(2):
-                h_codes[(h, G)] = keep.tile([P, HALF], U32, name="hc%d%d" % (h, G), align_bytes=64)
-                h_scales[(h, G)] = keep.tile([P, HALF], U8, name="hs%d%d" % (h, G), align_bytes=64)
+                h_codes[(h, G)] = keep.tile([P, HALF], U32, name="hc%d%d" % (h, G), align_bytes=256)
+                h_scales[(h, G)] = keep.tile([P, HALF], U8, name="hs%d%d" % (h, G), align_bytes=256)
         w_codes = {}
         w_scales = {}
         for w in range(4):
             for G in range(2):
-                w_codes[(w, G)] = keep.tile([P, 4, 2, P], U32, name="wc%d%d" % (w, G), align_bytes=64)
-                w_scales[(w, G)] = keep.tile([P, 4, 2, P], U8, name="ws%d%d" % (w, G), align_bytes=64)
+                w_codes[(w, G)] = keep.tile([P, 4, 2, P], U32, name="wc%d%d" % (w, G), align_bytes=256)
+                w_scales[(w, G)] = keep.tile([P, 4, 2, P], U8, name="ws%d%d" % (w, G), align_bytes=256)
 
         loads = [('w', 0, 0, 0), ('w', 0, 0, 1), ('a', 0, 0, 0), ('a', 0, 0, 1), ('w', 1, 0, 0), ('w', 1, 0, 1), ('a', 1, 0, 0), ('a', 1, 0, 1), ('w', 2, 0, 0), ('w', 2, 0, 1), ('a', 2, 0, 0), ('a', 2, 0, 1), ('w', 0, 1, 0), ('w', 0, 1, 1), ('w', 1, 1, 0), ('w', 1, 1, 1), ('a', 0, 1, 0), ('a', 0, 1, 1), ('w', 2, 1, 0), ('w', 2, 1, 1), ('a', 1, 1, 0), ('a', 1, 1, 1), ('a', 2, 1, 0), ('a', 2, 1, 1), ('i', 2, 0), ('i', 2, 1), ('w', 3, 0, 0), ('w', 3, 0, 1), ('w', 3, 1, 0), ('w', 3, 1, 1)]
         raws = {}
@@ -211,11 +211,14 @@ def tile_pt_grumb_pb_kernel(
 
         oacc = {}
 
-        def O(h, Go, jj, gs=(0, 1)):
+        def O(h, Go, jj, gs=(0, 1), bank="acc"):
             k = (h, Go, jj)
             for G in gs:
                 if G == 0:
-                    oacc[k] = psa.tile([P, HALF], F32, tag="acc", name="o_acc%d%d%d" % k)
+                    if bank == "T":
+                        oacc[k] = pst.tile([P, HALF], F32, tag="T", name="o_acc%d%d%d" % k)
+                    else:
+                        oacc[k] = psa.tile([P, HALF], F32, tag="acc", name="o_acc%d%d%d" % k)
                 nc.tensor.matmul_mx(
                     out=oacc[k][:],
                     lhsT=w_codes[(3, Go)][:, jj, G, :].bitcast(FP8X4),
@@ -231,8 +234,8 @@ def tile_pt_grumb_pb_kernel(
             nc.scalar.activation(out=o[:], in_=oacc[(h, Go, jj)][:], func=ACTF.Tanh)
             nc.sync.dma_start(out=out_v[Go, jj // 2, jj % 2][:, h * HALF:(h + 1) * HALF], in_=o[:])
 
-        def OY(h, Go, jj):
-            O(h, Go, jj)
+        def OY(h, Go, jj, bank="acc"):
+            O(h, Go, jj, (0, 1), bank)
             Y(h, Go, jj)
 
         pump()
@@ -257,7 +260,7 @@ def tile_pt_grumb_pb_kernel(
         A(1,0,0)
         Q(1,0,1)
         A(1,0,1)
-        T(2,0,0,0)
+        T(2,0,0)
         C(2,0,0)
         T(2,0,1)
         C(2,0,1)

@@ -32,12 +32,12 @@ def tile_pt_grumb_pb_kernel(
         ctx.enter_context(tc.manual_schedule())
         const = ctx.enter_context(tc.tile_pool(name="const", bufs=1))
         keep = ctx.enter_context(tc.tile_pool(name="keep", bufs=1))
-        rawp = ctx.enter_context(tc.tile_pool(name="rawp", bufs=14))
+        rawp = ctx.enter_context(tc.tile_pool(name="rawp", bufs=10))
         agp = ctx.enter_context(tc.tile_pool(name="agp", bufs=3))
         wgp = ctx.enter_context(tc.tile_pool(name="wgp", bufs=4))
         sp = ctx.enter_context(tc.tile_pool(name="sp", bufs=3))
         hgp = ctx.enter_context(tc.tile_pool(name="hgp", bufs=2))
-        op = ctx.enter_context(tc.tile_pool(name="op", bufs=6))
+        op = ctx.enter_context(tc.tile_pool(name="op", bufs=12))
         psa = ctx.enter_context(tc.psum_pool(name="psa", bufs=4))
         pst = ctx.enter_context(tc.psum_pool(name="pst", bufs=4))
 
@@ -78,7 +78,7 @@ def tile_pt_grumb_pb_kernel(
         def pump():
             while nxt[0] < len(loads):
                 key = loads[nxt[0]]
-                if key[0] != "i" and len(order) >= 14 and order[-14] not in used:
+                if key[0] != "i" and len(order) >= 10 and order[-10] not in used:
                     return
                 nxt[0] += 1
                 if key[0] == "i":
@@ -180,7 +180,35 @@ def tile_pt_grumb_pb_kernel(
                     stop=(w == 2 and g == 1),
                 )
 
+        def XH(w, G, h, c, bank):
+            for jj in ALL:
+                k = (h, G, jj, c)
+                if w == 0:
+                    if bank == "T":
+                        accs[k] = pst.tile([P, HALF], F32, tag="T", name="acc%d%d%d%d" % k)
+                    else:
+                        accs[k] = psa.tile([P, HALF], F32, tag="acc", name="acc%d%d%d%d" % k)
+                for g in range(2):
+                    nc.tensor.matmul_mx(
+                        out=accs[k][:, 0:256],
+                        lhsT=w_codes[(w, G)][:, jj, g, :].bitcast(FP8X4),
+                        lhsT_scale=w_scales[(w, G)][:, jj, g, :],
+                        rhs=a_codes[(w, h)][:, g, c * 256:(c + 1) * 256].bitcast(FP8X4),
+                        rhs_scale=a_scales[(w, h)][:, g, c * 256:(c + 1) * 256],
+                        start=(w == 0 and g == 0),
+                        stop=(w == 2 and g == 1),
+                    )
+
         ss = {}
+
+        def SH(h, G, c):
+            if (h, G) not in ss:
+                s = sp.tile([P, 4, HALF], F32, tag="s", name="s%d%d" % (h, G))
+                ss[(h, G)] = s
+            for jj in ALL:
+                nc.scalar.activation(
+                    out=ss[(h, G)][:, jj, c * 256:(c + 1) * 256], in_=accs[(h, G, jj, c)][:, 0:256], func=ACTF.Sigmoid
+                )
 
         def S(h, G, tiles=ALL):
             if (h, G) not in ss:
@@ -234,6 +262,35 @@ def tile_pt_grumb_pb_kernel(
             nc.scalar.activation(out=o[:], in_=oacc[(h, Go, jj)][:], func=ACTF.Tanh)
             nc.sync.dma_start(out=out_v[Go, jj // 2, jj % 2][:, h * HALF:(h + 1) * HALF], in_=o[:])
 
+        def OH(h, Go, jj, c, bank):
+            if bank == "T":
+                oh = pst.tile([P, HALF], F32, tag="T", name="oh%d%d%d%d" % (h, Go, jj, c))
+            else:
+                oh = psa.tile([P, HALF], F32, tag="acc", name="oh%d%d%d%d" % (h, Go, jj, c))
+            for G in range(2):
+                nc.tensor.matmul_mx(
+                    out=oh[:, 0:256],
+                    lhsT=w_codes[(3, Go)][:, jj, G, :].bitcast(FP8X4),
+                    lhsT_scale=w_scales[(3, Go)][:, jj, G, :],
+                    rhs=h_codes[(h, G)][:, c * 256:(c + 1) * 256].bitcast(FP8X4),
+                    rhs_scale=h_scales[(h, G)][:, c * 256:(c + 1) * 256],
+                    start=(G == 0),
+                    stop=(G == 1),
+                )
+            o = op.tile([P, 256], F32, tag="oh", bufs=12, name="o%d%d%d%d" % (h, Go, jj, c))
+            nc.scalar.activation(out=o[:], in_=oh[:, 0:256], func=ACTF.Tanh)
+            c0 = h * HALF + c * 256
+            nc.sync.dma_start(out=out_v[Go, jj // 2, jj % 2][:, c0:c0 + 256], in_=o[:])
+
+        def Y2(h, Go, jj):
+            o = op.tile([P, HALF], F32, tag="o", name="o%d%d%d" % (h, Go, jj))
+            for c in range(2):
+                nc.scalar.activation(out=o[:, c * 256:(c + 1) * 256], in_=oacc[(h, Go, jj)][:, c * 256:(c + 1) * 256], func=ACTF.Tanh)
+                nc.sync.dma_start(
+                    out=out_v[Go, jj // 2, jj % 2][:, h * HALF + c * 256:h * HALF + (c + 1) * 256],
+                    in_=o[:, c * 256:(c + 1) * 256],
+                )
+
         def OY(h, Go, jj, bank="acc"):
             O(h, Go, jj, (0, 1), bank)
             Y(h, Go, jj)
@@ -274,9 +331,9 @@ def tile_pt_grumb_pb_kernel(
         T(0,1,0)
         C(0,1,0)
         T(0,1,1)
+        C(0,1,1)
         X(2,0,0,LO)
         S(0,0,LO)
-        C(0,1,1)
         Q(0,1,0)
         Q(0,1,1)
         X(2,0,0,HI)

@@ -337,25 +337,27 @@ def tile_pt_grumb_pb_kernel(
         Q(0,1,0)
         Q(0,1,1)
         X(2,0,0,HI)
-        S(0,0,HI)
         T(1,1,0)
-        T(1,1,1)
         C(1,1,0)
-        C(1,1,1)
-        X(0,1,0)
+        S(0,0,HI)
+        X(0,1,0,LO)
         R(0,1,0,"V")
+        T(1,1,1)
+        C(1,1,1)
+        X(0,1,0,HI)
         Q(1,1,0)
-        Q(1,1,1)
         R(0,1,1,"V")
         T(2,1,0)
-        T(2,1,1)
         C(2,1,0)
-        C(2,1,1)
+        Q(1,1,1)
+        X(1,1,0,LO)
         A(0,1,0)
-        X(1,1,0)
+        T(2,1,1)
+        C(2,1,1)
+        X(1,1,0,HI)
         Q(2,1,0)
-        Q(2,1,1)
         A(0,1,1)
+        Q(2,1,1)
         R(1,1,0,"x320")
         R(1,1,1,"x320")
         X(2,1,0)
@@ -375,19 +377,21 @@ def tile_pt_grumb_pb_kernel(
         X(2,0,1)
         S(1,0)
         T(3,0,0)
-        C(3,0,0,"SS")
+        C(3,0,0)
+        X(0,1,1,LO)
         T(3,0,1)
-        C(3,0,1,"SS")
-        X(0,1,1)
-        H(1,0)
+        C(3,0,1)
+        X(0,1,1,HI)
         Q(3,0,0)
+        H(1,0)
         Q(3,0,1)
         K(1,0)
         T(3,1,0)
-        C(3,1,0,"SS")
+        C(3,1,0)
+        X(1,1,1,LO)
         T(3,1,1)
-        C(3,1,1,"SS")
-        X(1,1,1)
+        C(3,1,1)
+        X(1,1,1,HI)
         Q(3,1,0)
         Q(3,1,1)
         X(2,1,1)

@@ -337,27 +337,25 @@ def tile_pt_grumb_pb_kernel(
         Q(0,1,0)
         Q(0,1,1)
         X(2,0,0,HI)
-        T(1,1,0)
-        C(1,1,0)
         S(0,0,HI)
-        X(0,1,0,LO)
-        R(0,1,0,"V")
+        T(1,1,0)
         T(1,1,1)
+        C(1,1,0)
         C(1,1,1)
-        X(0,1,0,HI)
+        X(0,1,0)
+        R(0,1,0,"V")
         Q(1,1,0)
+        Q(1,1,1)
         R(0,1,1,"V")
         T(2,1,0)
-        C(2,1,0)
-        Q(1,1,1)
-        X(1,1,0,LO)
-        A(0,1,0)
         T(2,1,1)
+        C(2,1,0)
         C(2,1,1)
-        X(1,1,0,HI)
+        A(0,1,0)
+        X(1,1,0)
         Q(2,1,0)
-        A(0,1,1)
         Q(2,1,1)
+        A(0,1,1)
         R(1,1,0,"x320")
         R(1,1,1,"x320")
         X(2,1,0)

from contextlib import ExitStack

import concourse.mybir as mybir
from concourse.masks import make_identity

F32 = mybir.dt.float32
BF16 = mybir.dt.bfloat16
U32 = mybir.dt.uint32
U8 = mybir.dt.uint8
FP8X4 = mybir.dt.float8_e4m3fn_x4
ACTF = mybir.ActivationFunctionType
ALU = mybir.AluOpType
P = 128
HALF = 512
FLOPS = 4 * 2 * 1024 * 1024 * 1024
LO = (0, 1)
HI = (2, 3)
ALL = (0, 1, 2, 3)

def tile_pt_grumb_pb_kernel(
    tc, x, out0, mem0, inp_out, w_readgate, w_rec_readgate, w_mem_readgate, w_hid_out, out
):
    nc = tc.nc
    acts = [x, out0, mem0]
    weights = [w_readgate, w_rec_readgate, w_mem_readgate, w_hid_out]
    act_v = [a.rearrange("(g u p e) c -> g u p e c", g=2, u=2, e=2) for a in acts]
    w_v = [w.rearrange("(G U p E) k -> G U p (E k)", G=2, U=2, E=2) for w in weights]
    inp_v = inp_out.rearrange("(G U p E) c -> G U p (E c)", G=2, U=2, E=2)
    out_v = out.rearrange("(G U p E) c -> G U E p c", G=2, U=2, E=2)

    with ExitStack() as ctx:
        ctx.enter_context(tc.manual_schedule())
        const = ctx.enter_context(tc.tile_pool(name="const", bufs=1))
        keep = ctx.enter_context(tc.tile_pool(name="keep", bufs=1))
        rawp = ctx.enter_context(tc.tile_pool(name="rawp", bufs=10))
        agp = ctx.enter_context(tc.tile_pool(name="agp", bufs=3))
        wgp = ctx.enter_context(tc.tile_pool(name="wgp", bufs=4))
        sp = ctx.enter_context(tc.tile_pool(name="sp", bufs=3))
        hgp = ctx.enter_context(tc.tile_pool(name="hgp", bufs=2))
        op = ctx.enter_context(tc.tile_pool(name="op", bufs=12))
        psa = ctx.enter_context(tc.psum_pool(name="psa", bufs=4))
        pst = ctx.enter_context(tc.psum_pool(name="pst", bufs=4))

        ident = const.tile([P, P], F32, name="ident")
        make_identity(nc, ident[:])
        warm = const.tile([P, 8], F32, name="warm")
        nc.vector.memset(warm[:], 0.0)
        nc.scalar.activation(out=warm[:], in_=warm[:], func=ACTF.Sigmoid)

        dum = const.tile([P, HALF], BF16, name="dum")
        nc.vector.memset(dum[:], 0.0)
        inp = keep.tile([P, 2, 4, 1024], BF16, name="inp")
        a_codes = {}
        a_scales = {}
        h_codes = {}
        h_scales = {}
        for h in range(2):
            for a in range(3):
                a_codes[(a, h)] = keep.tile([P, 2, HALF], U32, name="ac%d%d" % (a, h), align_bytes=256)
                a_scales[(a, h)] = keep.tile([P, 2, HALF], U8, name="as%d%d" % (a, h), align_bytes=256)
            for G in range(2):
                h_codes[(h, G)] = keep.tile([P, HALF], U32, name="hc%d%d" % (h, G), align_bytes=256)
                h_scales[(h, G)] = keep.tile([P, HALF], U8, name="hs%d%d" % (h, G), align_bytes=256)
        w_codes = {}
        w_scales = {}
        for w in range(4):
            for G in range(2):
                w_codes[(w, G)] = keep.tile([P, 4, 2, P], U32, name="wc%d%d" % (w, G), align_bytes=256)
                w_scales[(w, G)] = keep.tile([P, 4, 2, P], U8, name="ws%d%d" % (w, G), align_bytes=256)

        loads = [('w', 0, 0, 0), ('w', 0, 0, 1), ('a', 0, 0, 0), ('a', 0, 0, 1), ('w', 1, 0, 0), ('w', 1, 0, 1), ('a', 1, 0, 0), ('a', 1, 0, 1), ('w', 2, 0, 0), ('w', 2, 0, 1), ('a', 2, 0, 0), ('a', 2, 0, 1), ('w', 0, 1, 0), ('w', 0, 1, 1), ('w', 1, 1, 0), ('w', 1, 1, 1), ('a', 0, 1, 0), ('a', 0, 1, 1), ('w', 2, 1, 0), ('w', 2, 1, 1), ('a', 1, 1, 0), ('a', 1, 1, 1), ('a', 2, 1, 0), ('a', 2, 1, 1), ('i', 2, 0), ('i', 2, 1), ('w', 3, 0, 0), ('w', 3, 0, 1), ('w', 3, 1, 0), ('w', 3, 1, 1)]
        raws = {}
        nxt = [0]

        order = []
        used = set()

        def pump():
            while nxt[0] < len(loads):
                key = loads[nxt[0]]
                if key[0] != "i" and len(order) >= 10 and order[-10] not in used:
                    return
                nxt[0] += 1
                if key[0] == "i":
                    i, G = key[1], key[2]
                    for U in range(2):
                        nc.sync.dma_start(
                            out=inp[:, G, 2 * U:2 * U + 2, :].rearrange("p t c -> p (t c)"),
                            in_=inp_v[G, U],
                        )
                    continue
                order.append(key)
                raw = rawp.tile([P, 2048], BF16, tag="raw", name="raw_%s%d%d%d" % key)
                raws[key] = raw
                kind, i, j, s = key
                if kind == "a":
                    for u in range(2):
                        nc.sync.dma_start(
                            out=raw[:, u * 2 * HALF:(u + 1) * 2 * HALF].rearrange("p (e c) -> p e c", e=2),
                            in_=act_v[i][s, u][:, :, j * HALF:(j + 1) * HALF],
                        )
                else:
                    nc.sync.dma_start(out=raw[:], in_=w_v[i][j, s])

        ags = {}

        def R(a, h, g, eng="V"):
            ag = agp.tile([P, 2048], BF16, tag="ag", name="ag%d%d%d" % (a, h, g), align_bytes=64)
            ags[(a, h, g)] = ag
            raw = raws[("a", a, h, g)]
            ends = {"V": ((0, HALF, "V"),), "S": ((0, HALF, "S"),)}
            for c0, c1, e in ends.get(eng) or ((0, int(eng[1:]), "V"), (int(eng[1:]), HALF, "S")):
                dst = ag[:, 4 * c0:4 * c1].rearrange("p (c i t) -> p c t i", i=4, t=4)
                src = raw[:].rearrange("p (t c) -> p t c", t=4)[:, :, c0:c1].rearrange("p t (c i) -> p c t i", i=4)
                if e == "S":
                    nc.scalar.copy(out=dst, in_=src)
                else:
                    nc.vector.tensor_copy(out=dst, in_=src)
            used.add(("a", a, h, g))
            pump()

        def A(a, h, g):
            nc.vector.quantize_mx(
                out=a_codes[(a, h)][:, g, :].bitcast(FP8X4),
                scales=a_scales[(a, h)][:, g, :],
                in_=ags[(a, h, g)][:],
            )

        tbs = {}

        def T(w, G, U, pre=0):
            words = raws[("w", w, G, U)][:].bitcast(F32)
            for E in range(2):
                tb = pst.tile([P, 4, P], F32, tag="T", name="tb%d%d%d%d" % (w, G, U, E))
                if E == 0:
                    for n in range(pre):
                        nc.tensor.matmul(out=tb[:].rearrange("p a m -> p (a m)"), lhsT=dum[:, 0:P], rhs=dum[:], start=True, stop=True)
                for b in range(4):
                    c0 = E * 512 + b * P
                    nc.tensor.transpose(tb[:, b, :], words[:, c0:c0 + P], ident[:])
                tbs[(w, G, U, E)] = tb
            used.add(("w", w, G, U))
            pump()

        wgs = {}

        def C(w, G, U, eng="SS"):
            wg = wgp.tile([P, 2048], BF16, tag="wg", name="wg%d%d%d" % (w, G, U), align_bytes=64)
            wgs[(w, G, U)] = wg
            wgf = wg[:].bitcast(F32).rearrange("p (a g m u) -> p a g m u", a=2, g=2, u=2)
            for E in range(2):
                bank = tbs[(w, G, U, E)][:].rearrange("p (g u) m -> p g m u", u=2)
                if eng[E] == "V":
                    nc.vector.tensor_copy(out=wgf[:, E], in_=bank)
                else:
                    nc.scalar.copy(out=wgf[:, E], in_=bank)

        def Q(w, G, U):
            nc.vector.quantize_mx(
                out=w_codes[(w, G)][:, 2 * U:2 * U + 2].rearrange("p a g m -> p (a g m)").bitcast(FP8X4),
                scales=w_scales[(w, G)][:, 2 * U:2 * U + 2].rearrange("p a g m -> p (a g m)"),
                in_=wgs[(w, G, U)][:],
            )

        accs = {}

        def X(w, G, h, tiles=ALL, gs=(0, 1), gouter=False):
            order = [(jj, g) for g in gs for jj in tiles] if gouter else [(jj, g) for jj in tiles for g in gs]
            for jj, g in order:
                k = (h, G, jj)
                if w == 0 and g == 0:
                    accs[k] = psa.tile([P, HALF], F32, tag="acc", name="acc%d%d%d" % k)
                nc.tensor.matmul_mx(
                    out=accs[k][:],
                    lhsT=w_codes[(w, G)][:, jj, g, :].bitcast(FP8X4),
                    lhsT_scale=w_scales[(w, G)][:, jj, g, :],
                    rhs=a_codes[(w, h)][:, g, :].bitcast(FP8X4),
                    rhs_scale=a_scales[(w, h)][:, g, :],
                    start=(w == 0 and g == 0),
                    stop=(w == 2 and g == 1),
                )

        def XH(w, G, h, c, bank):
            for jj in ALL:
                k = (h, G, jj, c)
                if w == 0:
                    if bank == "T":
                        accs[k] = pst.tile([P, HALF], F32, tag="T", name="acc%d%d%d%d" % k)
                    else:
                        accs[k] = psa.tile([P, HALF], F32, tag="acc", name="acc%d%d%d%d" % k)
                for g in range(2):
                    nc.tensor.matmul_mx(
                        out=accs[k][:, 0:256],
                        lhsT=w_codes[(w, G)][:, jj, g, :].bitcast(FP8X4),
                        lhsT_scale=w_scales[(w, G)][:, jj, g, :],
                        rhs=a_codes[(w, h)][:, g, c * 256:(c + 1) * 256].bitcast(FP8X4),
                        rhs_scale=a_scales[(w, h)][:, g, c * 256:(c + 1) * 256],
                        start=(w == 0 and g == 0),
                        stop=(w == 2 and g == 1),
                    )

        ss = {}

        def SH(h, G, c):
            if (h, G) not in ss:
                s = sp.tile([P, 4, HALF], F32, tag="s", name="s%d%d" % (h, G))
                ss[(h, G)] = s
            for jj in ALL:
                nc.scalar.activation(
                    out=ss[(h, G)][:, jj, c * 256:(c + 1) * 256], in_=accs[(h, G, jj, c)][:, 0:256], func=ACTF.Sigmoid
                )

        def S(h, G, tiles=ALL):
            if (h, G) not in ss:
                s = sp.tile([P, 4, HALF], F32, tag="s", name="s%d%d" % (h, G))
                ss[(h, G)] = s
            for jj in tiles:
                nc.scalar.activation(out=ss[(h, G)][:, jj, :], in_=accs[(h, G, jj)][:], func=ACTF.Sigmoid)

        hgs = {}

        def H(h, G, c0=0, c1=HALF):
            if (h, G) not in hgs:
                hg = hgp.tile([P, HALF, 4], BF16, tag="hg", name="hg%d%d" % (h, G), align_bytes=64)
                hgs[(h, G)] = hg
            nc.vector.tensor_tensor(
                out=hgs[(h, G)][:, c0:c1].rearrange("p (c i) t -> p c t i", i=4),
                in0=ss[(h, G)][:, :, c0:c1].rearrange("p t (c i) -> p c t i", i=4),
                in1=inp[:, G, :, h * HALF + c0:h * HALF + c1].rearrange("p t (c i) -> p c t i", i=4),
                op=ALU.add,
            )

        def K(h, G, c0=0, c1=HALF):
            nc.vector.quantize_mx(
                out=h_codes[(h, G)][:, c0:c1].bitcast(FP8X4),
                scales=h_scales[(h, G)][:, c0:c1],
                in_=hgs[(h, G)][:, c0:c1].rearrange("p c t -> p (c t)"),
            )

        oacc = {}

        def O(h, Go, jj, gs=(0, 1), bank="acc"):
            k = (h, Go, jj)
            for G in gs:
                if G == 0:
                    if bank == "T":
                        oacc[k] = pst.tile([P, HALF], F32, tag="T", name="o_acc%d%d%d" % k)
                    else:
                        oacc[k] = psa.tile([P, HALF], F32, tag="acc", name="o_acc%d%d%d" % k)
                nc.tensor.matmul_mx(
                    out=oacc[k][:],
                    lhsT=w_codes[(3, Go)][:, jj, G, :].bitcast(FP8X4),
                    lhsT_scale=w_scales[(3, Go)][:, jj, G, :],
                    rhs=h_codes[(h, G)][:].bitcast(FP8X4),
                    rhs_scale=h_scales[(h, G)][:],
                    start=(G == 0),
                    stop=(G == 1),
                )

        def Y(h, Go, jj):
            o = op.tile([P, HALF], F32, tag="o", name="o%d%d%d" % (h, Go, jj))
            nc.scalar.activation(out=o[:], in_=oacc[(h, Go, jj)][:], func=ACTF.Tanh)
            nc.sync.dma_start(out=out_v[Go, jj // 2, jj % 2][:, h * HALF:(h + 1) * HALF], in_=o[:])

        def OH(h, Go, jj, c, bank):
            if bank == "T":
                oh = pst.tile([P, HALF], F32, tag="T", name="oh%d%d%d%d" % (h, Go, jj, c))
            else:
                oh = psa.tile([P, HALF], F32, tag="acc", name="oh%d%d%d%d" % (h, Go, jj, c))
            for G in range(2):
                nc.tensor.matmul_mx(
                    out=oh[:, 0:256],
                    lhsT=w_codes[(3, Go)][:, jj, G, :].bitcast(FP8X4),
                    lhsT_scale=w_scales[(3, Go)][:, jj, G, :],
                    rhs=h_codes[(h, G)][:, c * 256:(c + 1) * 256].bitcast(FP8X4),
                    rhs_scale=h_scales[(h, G)][:, c * 256:(c + 1) * 256],
                    start=(G == 0),
                    stop=(G == 1),
                )
            o = op.tile([P, 256], F32, tag="oh", bufs=12, name="o%d%d%d%d" % (h, Go, jj, c))
            nc.scalar.activation(out=o[:], in_=oh[:, 0:256], func=ACTF.Tanh)
            c0 = h * HALF + c * 256
            nc.sync.dma_start(out=out_v[Go, jj // 2, jj % 2][:, c0:c0 + 256], in_=o[:])

        def Y2(h, Go, jj):
            o = op.tile([P, HALF], F32, tag="o", name="o%d%d%d" % (h, Go, jj))
            for c in range(2):
                nc.scalar.activation(out=o[:, c * 256:(c + 1) * 256], in_=oacc[(h, Go, jj)][:, c * 256:(c + 1) * 256], func=ACTF.Tanh)
                nc.sync.dma_start(
                    out=out_v[Go, jj // 2, jj % 2][:, h * HALF + c * 256:h * HALF + (c + 1) * 256],
                    in_=o[:, c * 256:(c + 1) * 256],
                )

        def OY(h, Go, jj, bank="acc"):
            O(h, Go, jj, (0, 1), bank)
            Y(h, Go, jj)

        pump()
        T(0,0,0,6)
        C(0,0,0)
        T(0,0,1)
        R(0,0,0,"x352")
        C(0,0,1)
        Q(0,0,0)
        R(0,0,1,"x352")
        A(0,0,0)
        Q(0,0,1)
        A(0,0,1)
        T(1,0,0,4)
        C(1,0,0)
        T(1,0,1)
        C(1,0,1)
        X(0,0,0,ALL,(0,1))
        R(1,0,0,"x352")
        Q(1,0,0)
        R(1,0,1,"x352")
        A(1,0,0)
        Q(1,0,1)
        A(1,0,1)
        T(2,0,0)
        C(2,0,0)
        T(2,0,1)
        C(2,0,1)
        X(1,0,0,ALL,(0,1))
        R(2,0,0,"x352")
        Q(2,0,0)
        R(2,0,1,"x352")
        A(2,0,0)
        Q(2,0,1)
        A(2,0,1)
        T(0,1,0)
        C(0,1,0)
        T(0,1,1)
        C(0,1,1)
        X(2,0,0,LO)
        S(0,0,LO)
        Q(0,1,0)
        Q(0,1,1)
        X(2,0,0,HI)
        S(0,0,HI)
        T(1,1,0)
        T(1,1,1)
        C(1,1,0)
        C(1,1,1)
        X(0,1,0)
        R(0,1,0,"V")
        Q(1,1,0)
        Q(1,1,1)
        R(0,1,1,"V")
        T(2,1,0)
        T(2,1,1)
        C(2,1,0)
        C(2,1,1)
        A(0,1,0)
        X(1,1,0)
        Q(2,1,0)
        Q(2,1,1)
        A(0,1,1)
        R(1,1,0,"x320")
        R(1,1,1,"x320")
        X(2,1,0)
        S(0,1)
        A(1,1,0)
        A(1,1,1)
        X(0,0,1)
        R(2,1,0,"x320")
        R(2,1,1,"x320")
        A(2,1,0)
        X(1,0,1)
        A(2,1,1)
        H(0,0)
        H(0,1)
        K(0,0)
        K(0,1)
        X(2,0,1)
        S(1,0)
        T(3,0,0)
        C(3,0,0)
        X(0,1,1,LO)
        T(3,0,1)
        C(3,0,1)
        X(0,1,1,HI)
        Q(3,0,0)
        H(1,0)
        Q(3,0,1)
        K(1,0)
        T(3,1,0)
        C(3,1,0)
        X(1,1,1,LO)
        T(3,1,1)
        C(3,1,1)
        X(1,1,1,HI)
        Q(3,1,0)
        Q(3,1,1)
        X(2,1,1)
        S(1,1)
        H(1,1)
        K(1,1)
        OY(0,0,0)
        OY(0,0,1)
        OY(0,0,2)
        OY(0,0,3)
        OY(0,1,0)
        OY(0,1,1)
        OY(0,1,2)
        OY(0,1,3)
        OY(1,0,0)
        OY(1,0,1)
        OY(1,0,2)
        OY(1,0,3)
        OY(1,1,0)
        OY(1,1,1)
        OY(1,1,2)
        OY(1,1,3)
